import numpy as np
import ml_dtypes


def mxq(x, axis, fmt="e4m3"):
    dtype, down = {"e4m3": (ml_dtypes.float8_e4m3fn, 7), "e5m2": (ml_dtypes.float8_e5m2, 14)}[fmt]
    v = np.moveaxis(np.asarray(x, np.float32).astype(ml_dtypes.bfloat16).astype(np.float64), axis, -1)
    blocks = v.reshape(v.shape[:-1] + (-1, 32))
    amax = np.abs(blocks).max(-1, keepdims=True)
    byte = np.maximum(np.where(amax > 0, np.frexp(amax)[1] - 1 + 127, 0) - down, 1)
    scale = np.exp2(byte - 127.0)
    codes = (blocks / scale).astype(np.float32).astype(dtype).astype(np.float64)
    return np.moveaxis((codes * scale).reshape(v.shape), -1, axis)


WIDE = False


def mx_kscale(k):
    if not WIDE:
        return np.ones(k)
    levels = np.array([10, -10, 5, -5, 0])
    if k % 512:
        return np.exp2(np.random.permutation(np.resize(levels, k // 32))).repeat(32)
    a = np.empty((k // 512, 16))
    for p in range(k // 512):
        a[p, :8] = np.random.permutation(np.resize(levels, 8))
        for g in range(8):
            far = levels[np.abs(levels - a[p, g]) >= 10]
            a[p, g + 8] = far[np.random.randint(len(far))]
    return np.exp2(a.ravel()).repeat(32)


BF16 = ml_dtypes.bfloat16


def bf(x):
    return np.asarray(x, np.float32).astype(BF16)


def f64(x):
    return np.asarray(x).astype(np.float64)


B, D_IN, D_OUT = 4096, 1024, 512
EPS = 0.01


def draw0():
    s, t = mx_kscale(D_IN), mx_kscale(D_OUT)
    return {"x": bf(np.random.standard_normal((B, D_IN)) * s),
            "W": bf(np.random.standard_normal((D_OUT, D_IN)) / np.sqrt(D_IN) / s[None, :] * t[:, None]),
            "b": bf(np.random.standard_normal(D_OUT) * 0.3 * t),
            "g": bf(np.random.standard_normal((D_OUT, D_OUT)) / np.sqrt(D_OUT) / t[None, :]),
            "g_bias": bf(np.random.standard_normal(D_OUT) * 0.3)}


def core(x, W, b, g, g_bias):
    h = (mxq(f64(x), 1, "e4m3") @ mxq(f64(W), 1, "e4m3").T) + f64(b)
    c = np.cos((mxq(h, 1, "e4m3") @ mxq(f64(g), 1, "e4m3").T) + f64(g_bias))
    return np.where(np.abs(c) < EPS, -c, c)


def e4m3fn_bytes(y):
    return np.clip(np.asarray(y, np.float64), -448.0, 448.0).astype(np.float32).astype(ml_dtypes.float8_e4m3fn).view(np.uint8)


def e4m3fn_values(b):
    return np.asarray(b, np.uint8).view(ml_dtypes.float8_e4m3fn).astype(np.float64)


def setup_inputs():
    d = draw0()
    x0 = np.asarray(d['x']).astype(np.float64)
    s = (np.max(np.abs(x0), axis=(0,), keepdims=True) / 448.0).astype(np.float32)
    out = {}
    for k, v in d.items():
        if k == 'x':
            out['x_bytes'] = e4m3fn_bytes(x0 / s.astype(np.float64))
            out['x_scale'] = s
        else:
            out[k] = v
    return out


def reference(x_bytes, x_scale, W, b, g, g_bias):
    return core(e4m3fn_values(x_bytes) * x_scale.astype(np.float64), W, b, g, g_bias)

import math
from contextlib import ExitStack

import concourse.mybir as mybir
from concourse.masks import make_identity

TOKENS, D_IN, D_OUT = 4096, 1024, 512
FLOPS = 2 * TOKENS * D_OUT * D_IN + 2 * TOKENS * D_OUT * D_OUT
EPS = 0.01

F32 = mybir.dt.float32
BF16 = mybir.dt.bfloat16
I32 = mybir.dt.int32
U32 = mybir.dt.uint32
U8 = mybir.dt.uint8
F8 = mybir.dt.float8_e4m3fn
F8X4 = mybir.dt.float8_e4m3fn_x4
ACT = mybir.ActivationFunctionType
ALU = mybir.AluOpType

P = 128
PASSES = D_IN // 512
TILES = D_OUT // P
CHUNKS = [512] * 8

HALVES = 2
ORDER = [
    ("TO", 0, 2),
    ("SN", 0, 2),
    ("TO", 1, 2),
    ("SN", 1, 2),
    ("SQ", 0, 2),
    ("QX", 0, 1),
    ("M1", 0, 1),
    ("HE", 0, 1),
    ("M1", 1, 1),
    ("HE", 1, 1),
    ("M1", 2, 1),
    ("HE", 2, 1),
    ("M1", 3, 1),
    ("HE", 3, 1),
    ("A", 0, 0),
    ("A", 1, 0),
    ("MK", 0, 2),
    ("F", 0, 2),
    ("IL", 0, 1),
    ("A", 2, 0),
    ("QH", 0, 1),
    ("TO", 2, 2),
    ("SN", 2, 2),
    ("TO", 3, 2),
    ("SN", 3, 2),
    ("SQ", 1, 2),
    ("MK", 1, 2),
    ("F", 1, 2),
    ("TX", 0, 0),
    ("XE", 0, 0),
    ("TX", 1, 0),
    ("XE", 1, 0),
    ("M2", 0, 1),
    ("WE", 0, 1),
    ("M2", 1, 1),
    ("WE", 1, 1),
    ("M2", 2, 1),
    ("WE", 2, 1),
    ("M2", 3, 1),
    ("WE", 3, 1),
    ("A", 3, 0),
    ("TX", 2, 0),
    ("XE", 2, 0),
    ("TX", 3, 0),
    ("XE", 3, 0),
    ("NN", 0, 1),
    ("NN", 1, 1),
    ("NF", 0, 1),
    ("NF", 1, 1),
]
SQ_SCALE = math.sqrt(1.0 + 2.0 ** -8) / EPS
SQ_LIMIT = 1.0 + 2.0 ** -8
TWO_PI = 2.0 * math.pi


def tile_onehiddenlayer_t_kernel(tc, x_bytes, x_scale, W, b, g, g_bias, out):
    nc = tc.nc
    starts = [sum(CHUNKS[:i]) for i in range(len(CHUNKS))]
    last = len(CHUNKS) - 1

    with ExitStack() as ctx:
        keep = ctx.enter_context(tc.tile_pool(name="keep", bufs=1))
        pool = ctx.enter_context(tc.tile_pool(name="pool", bufs=2))
        psum = ctx.enter_context(tc.psum_pool(name="psum", bufs=2))

        live = {}

        def load_x(i):
            n = CHUNKS[i]
            xb = pool.tile([P, n // P, D_IN], U8, tag="xb", bufs=4, align_bytes=64, name="xb")
            nc.sync.dma_start(out=xb[:], in_=x_bytes[starts[i]:starts[i] + n, :].rearrange("(p a) k -> p a k", p=P))
            live["xb", i] = xb

        spread = keep.tile([P, D_IN], F32, align_bytes=64, name="spread")
        nc.scalar.dma_start(out=spread[:], in_=x_scale.rearrange("o k -> (o k)").partition_broadcast(P))
        b_cols = keep.tile([P, TILES], BF16, name="b_cols")
        nc.scalar.dma_start(out=b_cols[:], in_=b.rearrange("(p t) -> p t", t=TILES))
        gb_cols = keep.tile([P, TILES], BF16, name="gb_cols")
        nc.scalar.dma_start(out=gb_cols[:], in_=g_bias.rearrange("(p t) -> p t", t=TILES))
        load_x(0)
        w_rows = W.rearrange("(m t) k -> m t k", t=TILES)
        w_raw = []
        for s in range(PASSES):
            raw = keep.tile([P, TILES, 512], BF16, align_bytes=64, name="w_raw%d" % s)
            nc.sync.dma_start(out=raw[:], in_=w_rows[:, :, s * 512:(s + 1) * 512])
            w_raw.append(raw)
        g_raw = keep.tile([P, TILES, 512], BF16, align_bytes=64, name="g_raw")
        nc.sync.dma_start(out=g_raw[:], in_=g.rearrange("(m t) k -> m t k", t=TILES))
        for i in range(1, min(4, len(CHUNKS))):
            load_x(i)

        ident = keep.tile([P, P], F32, name="ident")
        make_identity(nc, ident[:])
        phase = keep.tile([P, TILES], F32, name="phase")
        warm = keep.tile([P, 1], F32, name="warm")
        nc.vector.memset(warm[:], 0.0)
        nc.scalar.activation(out=warm[:], in_=warm[:], func=ACT.Sin)
        nc.vector.tensor_scalar(out=phase[:], in0=gb_cols[:], scalar1=1.0 / TWO_PI, scalar2=0.25, op0=ALU.mult, op1=ALU.add)

        w_codes = keep.tile([P, PASSES, D_OUT], U32, align_bytes=64, name="w_codes")
        w_scales = keep.tile([P, PASSES, D_OUT], U8, align_bytes=64, name="w_scales")
        g_codes = keep.tile([P, D_OUT], U32, align_bytes=64, name="g_codes")
        g_scales = keep.tile([P, D_OUT], U8, align_bytes=64, name="g_scales")

        def weight_pairs(raw, pairs):
            words = raw[:].rearrange("p t k -> p (t k)").bitcast(F32).rearrange("p (t w) -> p t w", t=TILES)
            view = pairs[:].bitcast(F32).rearrange("p (h a r u) -> p h a r u", h=2, a=2, u=2)
            for half in range(2):
                bank = psum.tile([P, 2, 2, P], F32, tag="acc", bufs=4, name="w_bank")
                for a in range(2):
                    for u in range(2):
                        nc.tensor.transpose(bank[:, a, u, :], words[:, 2 * half + a, u:256:2], ident[:])
                source = bank[:].rearrange("p a u r -> p a r u")
                nc.scalar.copy(out=view[:, half], in_=source)

        def weight_quantize(pairs, codes, scales):
            nc.vector.quantize_mx(out=codes.bitcast(F8X4), scales=scales, in_=pairs[:])

        def A(i, a):
            xs = pool.tile([P, D_IN], BF16, tag="xs", bufs=6, align_bytes=64, name="xs")
            nc.vector.tensor_tensor(out=xs[:], in0=live["xb", i][:, a, :].bitcast(F8), in1=spread[:], op=ALU.mult)
            live["xs", i, a] = xs

        def TX(i, a):
            words = live["xs", i, a][:].bitcast(F32)
            bank = psum.tile([P, PASSES, 2, P], F32, tag="xbank", bufs=2, name="xbank")
            for s in range(PASSES):
                for u in range(2):
                    nc.tensor.transpose(bank[:, s, u, :], words[:, 256 * s + u:256 * (s + 1):2], ident[:])
            live["xbank", i, a] = bank

        def XE(i, a):
            n = CHUNKS[i]
            if a == 0:
                xg = pool.tile([P, PASSES * n * 4], BF16, tag="xg", align_bytes=64, name="xg")
                live["xg", i] = xg
            view = live["xg", i][:].bitcast(F32).rearrange("p (s r u) -> p s r u", s=PASSES, u=2)
            nc.scalar.copy(out=view[:, :, a * P:(a + 1) * P, :], in_=live["xbank", i, a][:].rearrange("p s u r -> p s r u"))

        def QX(i, z):
            n = CHUNKS[i]
            codes = pool.tile([P, PASSES * n], U32, tag="xcodes", align_bytes=64, name="xcodes")
            scales = pool.tile([P, PASSES * n], U8, tag="xscales", align_bytes=64, name="xscales")
            nc.vector.quantize_mx(out=codes[:].bitcast(F8X4), scales=scales[:], in_=live["xg", i][:])
            live["xq", i] = codes, scales

        def M1(i, t):
            n = CHUNKS[i]
            codes, scales = live["xq", i]
            acc = psum.tile([P, n], F32, tag="acc", bufs=4, name="acc")
            for s in range(PASSES):
                nc.tensor.matmul_mx(
                    out=acc[:],
                    lhsT=w_codes[:, s, t * P:(t + 1) * P].bitcast(F8X4),
                    lhsT_scale=w_scales[:, s, t * P:(t + 1) * P],
                    rhs=codes[:, s * n:(s + 1) * n].bitcast(F8X4),
                    rhs_scale=scales[:, s * n:(s + 1) * n],
                    start=(s == 0),
                    stop=(s == PASSES - 1),
                )
            live["acc1", i, t] = acc

        def HE(i, t):
            if t == 0:
                ht = pool.tile([P, TILES, CHUNKS[i]], BF16, tag="ht", align_bytes=64, name="ht")
                live["ht", i] = ht
            nc.scalar.activation(out=live["ht", i][:, t, :], in_=live["acc1", i, t][:], func=ACT.Identity, bias=b_cols[:, t:t + 1])

        def IL(i, z):
            hg = pool.tile([P, CHUNKS[i] * 4], BF16, tag="hg", align_bytes=64, name="hg")
            nc.vector.tensor_copy(out=hg[:].rearrange("p (n t) -> p n t", t=TILES), in_=live["ht", i][:].rearrange("p t n -> p n t"))
            live["hg", i] = hg

        def QH(i, z):
            n = CHUNKS[i]
            codes = pool.tile([P, n], U32, tag="hcodes", align_bytes=64, name="hcodes")
            scales = pool.tile([P, n], U8, tag="hscales", align_bytes=64, name="hscales")
            nc.vector.quantize_mx(out=codes[:].bitcast(F8X4), scales=scales[:], in_=live["hg", i][:])
            live["hq", i] = codes, scales

        def M2(i, t):
            codes, scales = live["hq", i]
            acc = psum.tile([P, CHUNKS[i]], F32, tag="acc", bufs=4, name="acc")
            nc.tensor.matmul_mx(
                out=acc[:],
                lhsT=g_codes[:, t * P:(t + 1) * P].bitcast(F8X4),
                lhsT_scale=g_scales[:, t * P:(t + 1) * P],
                rhs=codes[:].bitcast(F8X4),
                rhs_scale=scales[:],
                start=True,
                stop=True,
            )
            live["acc2", i, t] = acc

        def WE(i, t):
            if t == 0:
                turns = pool.tile([P, TILES, CHUNKS[i]], F32, tag="turns", name="turns")
                live["turns", i] = turns
            nc.scalar.activation(out=live["turns", i][:, t, :], in_=live["acc2", i, t][:], func=ACT.Identity, bias=phase[:, t:t + 1], scale=1.0 / TWO_PI)

        def cols(i, h):
            half = CHUNKS[i] // HALVES
            return slice(h * half, (h + 1) * half)

        def NN(i, h):
            if h == 0:
                whole = pool.tile([P, TILES, CHUNKS[i]], I32, tag="whole", bufs=1, name="whole")
                live["whole", i] = whole
            nc.vector.tensor_copy(out=live["whole", i][:, :, cols(i, h)], in_=live["turns", i][:, :, cols(i, h)])

        def NF(i, h):
            if h == 0:
                minus = pool.tile([P, TILES, CHUNKS[i]], F32, tag="minus", name="minus")
                live["minus", i] = minus
            nc.vector.tensor_scalar(out=live["minus", i][:, :, cols(i, h)], in0=live["whole", i][:, :, cols(i, h)], scalar1=-1.0, scalar2=None, op0=ALU.mult)

        def TO(i, a):
            bank = psum.tile([P, TILES, P], F32, tag="obank", bufs=2, name="obank")
            for t in range(TILES):
                nc.tensor.matmul(bank[:, t, :], live["turns", i][:, t, a * P:(a + 1) * P], ident[:], is_transpose=True, start=True, stop=False)
                nc.tensor.matmul(bank[:, t, :], live["minus", i][:, t, a * P:(a + 1) * P], ident[:], is_transpose=True, start=False, stop=True)
            live["obank", i, a] = bank

        def SN(i, a):
            if a == 0:
                c = pool.tile([P, CHUNKS[i] // P, D_OUT], F32, tag="c", bufs=3, name="c")
                live["c", i] = c
            nc.scalar.activation(
                out=live["c", i][:, a, :].rearrange("p (m t) -> p m t", t=TILES),
                in_=live["obank", i, a][:].rearrange("p t m -> p m t"), func=ACT.Sin, scale=TWO_PI)

        def SQ(i, h):
            half = CHUNKS[i] // P // HALVES
            q = pool.tile([P, half * D_OUT], BF16, tag="q", bufs=4, name="q")
            nc.scalar.activation(out=q[:], in_=live["c", i][:, h * half:(h + 1) * half, :].rearrange("p a m -> p (a m)"), func=ACT.Square, scale=SQ_SCALE)
            live["q", i, h] = q

        def MK(i, h):
            half = CHUNKS[i] // P // HALVES
            near = pool.tile([P, half * D_OUT], BF16, tag="near", bufs=2, name="near")
            nc.vector.tensor_scalar(out=near[:], in0=live["q", i, h][:], scalar1=SQ_LIMIT, scalar2=-2.0, op0=ALU.is_lt, op1=ALU.mult)
            live["near", i, h] = near

        def F(i, h):
            half = CHUNKS[i] // P // HALVES
            rows = slice(h * half, (h + 1) * half)
            c = live["c", i][:, rows, :]
            flat = c.rearrange("p a m -> p (a m)")
            nc.vector.scalar_tensor_tensor(out=flat, in0=live["near", i, h][:], scalar=1.0, in1=flat, op0=ALU.add, op1=ALU.mult)
            n = CHUNKS[i]
            nc.sync.dma_start(out=out[starts[i]:starts[i] + n, :].rearrange("(p a) m -> p a m", p=P)[:, rows, :], in_=c)

        w_pairs = []
        for s in range(PASSES):
            pairs = keep.tile([P, D_OUT * 4], BF16, align_bytes=64, name="w_pairs%d" % s)
            weight_pairs(w_raw[s], pairs)
            w_pairs.append(pairs)
        g_pairs = keep.tile([P, D_OUT * 4], BF16, align_bytes=64, name="g_pairs")
        run = {"A": A, "TX": TX, "XE": XE, "QX": QX, "M1": M1, "HE": HE, "IL": IL, "QH": QH, "M2": M2, "WE": WE, "NN": NN, "NF": NF, "TO": TO, "SN": SN, "SQ": SQ, "MK": MK, "F": F}
        done = []
        lag = max(o for _, _, o in ORDER)
        for step in range(len(CHUNKS) + lag):
            for op, ix, off in ORDER:
                i = step - off
                blocks = CHUNKS[i] // P if 0 <= i < len(CHUNKS) else 0
                count = blocks if op in ("A", "TX", "XE", "TO", "SN") else HALVES if op in ("NN", "NF", "SQ", "MK", "F") else TILES
                if blocks == 0 or ix >= count:
                    continue
                if op == "QX" and i == 0:
                    for s in range(PASSES):
                        weight_quantize(w_pairs[s], w_codes[:, s, :], w_scales[:, s, :])
                if op == "IL" and i == 0:
                    weight_pairs(g_raw, g_pairs)
                    weight_quantize(g_pairs, g_codes[:], g_scales[:])
                if op == "A" and ix == 0 and i > 0 and ("xb", i) not in live:
                    load_x(i)
                run[op](i, ix)
